import numpy as np
import ml_dtypes


def mxq(x, axis, fmt="e4m3"):
    dtype, down = {"e4m3": (ml_dtypes.float8_e4m3fn, 7), "e5m2": (ml_dtypes.float8_e5m2, 14)}[fmt]
    v = np.moveaxis(np.asarray(x, np.float32).astype(ml_dtypes.bfloat16).astype(np.float64), axis, -1)
    blocks = v.reshape(v.shape[:-1] + (-1, 32))
    amax = np.abs(blocks).max(-1, keepdims=True)
    byte = np.maximum(np.where(amax > 0, np.frexp(amax)[1] - 1 + 127, 0) - down, 1)
    scale = np.exp2(byte - 127.0)
    codes = (blocks / scale).astype(np.float32).astype(dtype).astype(np.float64)
    return np.moveaxis((codes * scale).reshape(v.shape), -1, axis)


WIDE = False


def mx_kscale(k):
    if not WIDE:
        return np.ones(k)
    levels = np.array([10, -10, 5, -5, 0])
    a = np.random.permutation(np.resize(levels, k // 512 * 4)).reshape(k // 512, 4)
    idx = np.arange(k)
    return np.exp2(a[idx // 512, idx % 128 // 32])


BF16 = ml_dtypes.bfloat16


def bf(x):
    return np.asarray(x, np.float32).astype(BF16)


def f64(x):
    return np.asarray(x).astype(np.float64)


T, B, D, H, HD, A = 512, 1, 1024, 16, 128, 128
HH = H * HD
HA = H * A
N = HH + HH + HA + HA
EPS = 1e-5
QK = 1.5


def layer_norm(x, w, b):
    mu = x.mean(-1, keepdims=True)
    var = np.square(x - mu).mean(-1, keepdims=True)
    return (x - mu) * (1.0 / np.sqrt(var + EPS)) * w + b


def setup_inputs():
    s = mx_kscale(D)
    col = np.concatenate([np.ones(HH + HH), QK * np.ones(HA + HA)])
    return {"src": bf(np.random.standard_normal((T, B, D))),
            "ln1_w": bf((1.0 + 0.1 * np.random.standard_normal(D)) * s),
            "ln1_b": bf(0.1 * np.random.standard_normal(D) * s),
            "w_uvqk": bf(np.random.standard_normal((D, N)) * col / np.sqrt(D) / s[:, None]),
            "b_uvqk": bf(0.1 * np.random.standard_normal(N))}


def reference(src, ln1_w, ln1_b, w_uvqk, b_uvqk):
    src_norm = layer_norm(f64(src), f64(ln1_w), f64(ln1_b))
    return (mxq(src_norm, 2, "e4m3") @ mxq(f64(w_uvqk), 0, "e4m3")) + f64(b_uvqk)

@@ -1,0 +1,230 @@
+from contextlib import ExitStack
+
+import concourse.mybir as mybir
+from concourse.masks import make_identity
+
+F32 = mybir.dt.float32
+BF16 = mybir.dt.bfloat16
+U32 = mybir.dt.uint32
+U8 = mybir.dt.uint8
+FP8X4 = mybir.dt.float8_e4m3fn_x4
+ALU = mybir.AluOpType
+ACT = mybir.ActivationFunctionType
+
+P = 128
+PACK = 4
+T = 512
+D = 1024
+N = 8192
+EPS = 1e-5
+PASSES = D // (P * PACK)
+GROUPS = PASSES * PACK
+TOKEN_TILES = T // P
+N_TILE = 512
+LOAD_COLS = 1024
+LAST_CHUNK = N // LOAD_COLS - 1
+RUN = 4
+BN_FMAX = 512
+BN_STATS_DIM = 6
+BN_AGGR_DIM = 2
+VECTOR_EVERY = 4
+BIAS_ROWS = N // N_TILE
+
+FLOPS = 2 * T * D * N
+
+
+def regroup(engine_copy, grouped, rows):
+    engine_copy(
+        out=grouped.rearrange("p (q i) t -> p q t i", i=RUN),
+        in_=rows.rearrange("p t (q i) -> p q t i", i=RUN),
+    )
+
+
+def tile_stulayer_pa_kernel(tc, src, ln1_w, ln1_b, w_uvqk, b_uvqk, out):
+    nc = tc.nc
+    src_rows = src.rearrange("t b d -> (t b) d")
+    out_rows = out.rearrange("t b n -> (t b) n")
+    w_view = w_uvqk.rearrange("(c t p) n -> p c t n", c=PASSES, t=PACK, p=P)
+
+    with ExitStack() as ctx:
+        keep = ctx.enter_context(tc.tile_pool(name="keep", bufs=1))
+        raw_pool = ctx.enter_context(tc.tile_pool(name="raw", bufs=10))
+        grouped_pool = ctx.enter_context(tc.tile_pool(name="grouped", bufs=6))
+        code_pool = ctx.enter_context(tc.tile_pool(name="codes", bufs=8))
+        stage_pool = ctx.enter_context(tc.tile_pool(name="stage", bufs=2 * TOKEN_TILES))
+        psum = ctx.enter_context(tc.psum_pool(name="psum", bufs=8))
+
+        ln_rows = keep.tile([P, P], BF16)
+        nc.vector.memset(ln_rows[:], 0.0)
+        bias_rows = keep.tile([P, N_TILE], BF16)
+        nc.vector.memset(bias_rows[:], 0.0)
+        nc.sync.dma_start(
+            out=bias_rows[0:BIAS_ROWS, :], in_=b_uvqk.rearrange("(r n) -> r n", n=N_TILE)
+        )
+        nc.sync.dma_start(out=ln_rows[0:GROUPS, :], in_=ln1_w.rearrange("(g p) -> g p", p=P))
+        nc.sync.dma_start(
+            out=ln_rows[GROUPS : 2 * GROUPS, :], in_=ln1_b.rearrange("(g p) -> g p", p=P)
+        )
+        x_tiles = []
+        for i in range(TOKEN_TILES):
+            x_i = keep.tile([P, D], BF16, name="x%d" % i)
+            nc.sync.dma_start(out=x_i[:], in_=src_rows[i * P : (i + 1) * P, :])
+            x_tiles.append(x_i)
+
+        ident_bf = keep.tile([P, P], BF16)
+        make_identity(nc, ident_bf[:])
+        ident = keep.tile([P, P], F32)
+        make_identity(nc, ident[:])
+        eps_col = keep.tile([P, 1], F32)
+        nc.vector.memset(eps_col[:], EPS)
+
+        ln_cols_ps = psum.tile([P, P], BF16, tag="bank")
+        nc.tensor.transpose(ln_cols_ps[:], ln_rows[:], ident_bf[:])
+        gain_shift = keep.tile([P, 2 * GROUPS], F32)
+        nc.vector.tensor_copy(out=gain_shift[:], in_=ln_cols_ps[:, 0 : 2 * GROUPS])
+
+        bias_all = keep.tile([P, N], BF16)
+        for pair in range(BIAS_ROWS // 2):
+            bias_ps = psum.tile([P, 2 * N_TILE], BF16, tag="bank")
+            for half in range(2):
+                r = 2 * pair + half
+                nc.tensor.matmul(
+                    out=bias_ps[:, half * N_TILE : (half + 1) * N_TILE],
+                    lhsT=ident_bf[:, r : r + 1].to_broadcast([P, P]),
+                    rhs=bias_rows[:],
+                    start=True,
+                    stop=True,
+                )
+            nc.scalar.copy(
+                out=bias_all[:, pair * 2 * N_TILE : (pair + 1) * 2 * N_TILE], in_=bias_ps[:]
+            )
+
+        stats = keep.tile([P, TOKEN_TILES, D // BN_FMAX, BN_STATS_DIM], F32)
+        mean_var = keep.tile([P, TOKEN_TILES, BN_AGGR_DIM], F32)
+        for i in range(TOKEN_TILES):
+            for h in range(D // BN_FMAX):
+                nc.vector.bn_stats(
+                    out=stats[:, i, h, :], in_=x_tiles[i][:, h * BN_FMAX : (h + 1) * BN_FMAX]
+                )
+            nc.vector.bn_aggr(
+                out=mean_var[:, i, :], in_=stats[:, i, :, :].rearrange("p h s -> p (h s)")
+            )
+        std = keep.tile([P, TOKEN_TILES], F32)
+        nc.scalar.activation(
+            out=std[:], in_=mean_var[:, :, 1], func=ACT.Sqrt, bias=eps_col[:, 0:1], scale=1.0
+        )
+        rstd = keep.tile([P, TOKEN_TILES], F32)
+        nc.vector.reciprocal(out=rstd[:], in_=std[:])
+        neg_mean = keep.tile([P, TOKEN_TILES], F32)
+        nc.vector.tensor_scalar(
+            out=neg_mean[:], in0=mean_var[:, :, 0], scalar1=-1.0, scalar2=None, op0=ALU.mult
+        )
+
+        xhat_tiles = []
+        for i in range(TOKEN_TILES):
+            xhat_i = keep.tile([P, D], F32, name="xhat%d" % i)
+            engine = nc.vector if i % 2 == 0 else nc.gpsimd
+            engine.tensor_scalar(
+                out=xhat_i[:],
+                in0=x_tiles[i][:],
+                scalar1=neg_mean[:, i : i + 1],
+                scalar2=rstd[:, i : i + 1],
+                op0=ALU.add,
+                op1=ALU.mult,
+            )
+            xhat_tiles.append(xhat_i)
+
+        x_norm = keep.tile([P, GROUPS, T], BF16)
+        for g in range(GROUPS):
+            xt = psum.tile([P, T], F32, tag="bank")
+            for i in range(TOKEN_TILES):
+                nc.tensor.transpose(
+                    xt[:, i * P : (i + 1) * P], xhat_tiles[i][:, g * P : (g + 1) * P], ident[:]
+                )
+            gain = gain_shift[:, g : g + 1]
+            shift = gain_shift[:, GROUPS + g : GROUPS + g + 1]
+            if g % 2 == 0:
+                nc.scalar.activation(
+                    out=x_norm[:, g, :], in_=xt[:], func=ACT.Identity, scale=gain, bias=shift
+                )
+            else:
+                nc.vector.tensor_scalar(
+                    out=x_norm[:, g, :], in0=xt[:], scalar1=gain, scalar2=shift,
+                    op0=ALU.mult, op1=ALU.add,
+                )
+
+        x_grouped = keep.tile([P, PASSES, T, PACK], BF16, align_bytes=64)
+        for c in range(PASSES):
+            regroup(
+                nc.vector.tensor_copy,
+                x_grouped[:, c, :, :],
+                x_norm[:, c * PACK : (c + 1) * PACK, :],
+            )
+        x_codes = keep.tile([P, PASSES * T], U32, align_bytes=64)
+        x_scales = keep.tile([P, PASSES * T], U8, align_bytes=64)
+        nc.vector.quantize_mx(
+            out=x_codes[:].bitcast(FP8X4),
+            scales=x_scales[:],
+            in_=x_grouped[:].rearrange("p c n t -> p (c n t)"),
+        )
+
+        for chunk in range(N // LOAD_COLS):
+            chunk_cols = slice(chunk * LOAD_COLS, (chunk + 1) * LOAD_COLS)
+            raw = []
+            for c in range(PASSES):
+                raw_c = raw_pool.tile([P, PACK, LOAD_COLS], BF16, name="raw_c", tag="raw")
+                nc.sync.dma_start(out=raw_c[:], in_=w_view[:, c, :, chunk_cols])
+                raw.append(raw_c)
+            stages = []
+            for i in range(TOKEN_TILES):
+                stage_i = stage_pool.tile([P, LOAD_COLS], F32, name="stage_i", tag="stage")
+                stages.append(stage_i)
+
+            for part in range(LOAD_COLS // N_TILE):
+                local = slice(part * N_TILE, (part + 1) * N_TILE)
+                first = chunk * LOAD_COLS + part * N_TILE
+                accs = []
+                for i in range(TOKEN_TILES):
+                    acc_i = psum.tile([P, N_TILE], F32, name="acc_i", tag="bank")
+                    accs.append(acc_i)
+                for c in range(PASSES):
+                    w_grouped = grouped_pool.tile([P, N_TILE, PACK], BF16, align_bytes=64)
+                    if c == PASSES - 1 and (first // N_TILE) % VECTOR_EVERY == VECTOR_EVERY - 1:
+                        regroup(nc.vector.tensor_copy, w_grouped[:], raw[c][:, :, local])
+                    else:
+                        regroup(nc.scalar.copy, w_grouped[:], raw[c][:, :, local])
+                    w_codes = code_pool.tile([P, N_TILE], U32, align_bytes=64)
+                    w_scales = code_pool.tile([P, N_TILE], U8, align_bytes=64)
+                    nc.vector.quantize_mx(
+                        out=w_codes[:].bitcast(FP8X4),
+                        scales=w_scales[:],
+                        in_=w_grouped[:].rearrange("p n t -> p (n t)"),
+                    )
+                    for i in range(TOKEN_TILES):
+                        tokens = slice(c * T + i * P, c * T + (i + 1) * P)
+                        nc.tensor.matmul_mx(
+                            out=accs[i][:],
+                            lhsT=x_codes[:, tokens].bitcast(FP8X4),
+                            lhsT_scale=x_scales[:, tokens],
+                            rhs=w_codes[:].bitcast(FP8X4),
+                            rhs_scale=w_scales[:],
+                            start=(c == 0),
+                            stop=(c == PASSES - 1),
+                        )
+                for i in range(TOKEN_TILES):
+                    nc.vector.tensor_tensor(
+                        out=stages[i][:, local],
+                        in0=accs[i][:],
+                        in1=bias_all[:, first : first + N_TILE],
+                        op=ALU.add,
+                    )
+                    if chunk == LAST_CHUNK:
+                        nc.sync.dma_start(
+                            out=out_rows[i * P : (i + 1) * P, first : first + N_TILE],
+                            in_=stages[i][:, local],
+                        )
+            if chunk != LAST_CHUNK:
+                for i in range(TOKEN_TILES):
+                    nc.sync.dma_start(
+                        out=out_rows[i * P : (i + 1) * P, chunk_cols], in_=stages[i][:]
+                    )

@@ -21,14 +21,16 @@ PASSES = D // (P * PACK)
 GROUPS = PASSES * PACK
 TOKEN_TILES = T // P
 N_TILE = 512
+PARTS = N // N_TILE
 LOAD_COLS = 1024
-LAST_CHUNK = N // LOAD_COLS - 1
+CHUNKS = N // LOAD_COLS
+PARTS_PER_CHUNK = LOAD_COLS // N_TILE
+CHUNKS_AHEAD = 5
 RUN = 4
+VECTOR_EVERY = 4
 BN_FMAX = 512
 BN_STATS_DIM = 6
 BN_AGGR_DIM = 2
-VECTOR_EVERY = 4
-BIAS_ROWS = N // N_TILE
 
 FLOPS = 2 * T * D * N
 
@@ -48,18 +50,31 @@ def tile_stulayer_pa_kernel(tc, src, ln1_w, ln1_b, w_uvqk, b_uvqk, out):
 
     with ExitStack() as ctx:
         keep = ctx.enter_context(tc.tile_pool(name="keep", bufs=1))
-        raw_pool = ctx.enter_context(tc.tile_pool(name="raw", bufs=10))
+        raw_pool = ctx.enter_context(tc.tile_pool(name="raw", bufs=CHUNKS_AHEAD * PASSES))
         grouped_pool = ctx.enter_context(tc.tile_pool(name="grouped", bufs=6))
         code_pool = ctx.enter_context(tc.tile_pool(name="codes", bufs=8))
         stage_pool = ctx.enter_context(tc.tile_pool(name="stage", bufs=2 * TOKEN_TILES))
         psum = ctx.enter_context(tc.psum_pool(name="psum", bufs=8))
+        ctx.enter_context(tc.manual_schedule())
+
+        raw = {}
+
+        def load_chunk(chunk):
+            for c in range(PASSES):
+                raw_c = raw_pool.tile([P, PACK, LOAD_COLS], BF16, name="raw_c", tag="raw")
+                nc.sync.dma_start(
+                    out=raw_c[:], in_=w_view[:, c, :, chunk * LOAD_COLS : (chunk + 1) * LOAD_COLS]
+                )
+                raw[(chunk, c)] = raw_c
 
         ln_rows = keep.tile([P, P], BF16)
         nc.vector.memset(ln_rows[:], 0.0)
         bias_rows = keep.tile([P, N_TILE], BF16)
         nc.vector.memset(bias_rows[:], 0.0)
+        eps_col = keep.tile([P, 1], F32)
+        nc.vector.memset(eps_col[:], EPS)
         nc.sync.dma_start(
-            out=bias_rows[0:BIAS_ROWS, :], in_=b_uvqk.rearrange("(r n) -> r n", n=N_TILE)
+            out=bias_rows[0:PARTS, :], in_=b_uvqk.rearrange("(r n) -> r n", n=N_TILE)
         )
         nc.sync.dma_start(out=ln_rows[0:GROUPS, :], in_=ln1_w.rearrange("(g p) -> g p", p=P))
         nc.sync.dma_start(
@@ -70,13 +85,13 @@ def tile_stulayer_pa_kernel(tc, src, ln1_w, ln1_b, w_uvqk, b_uvqk, out):
             x_i = keep.tile([P, D], BF16, name="x%d" % i)
             nc.sync.dma_start(out=x_i[:], in_=src_rows[i * P : (i + 1) * P, :])
             x_tiles.append(x_i)
+        for chunk in range(CHUNKS_AHEAD):
+            load_chunk(chunk)
 
         ident_bf = keep.tile([P, P], BF16)
         make_identity(nc, ident_bf[:])
         ident = keep.tile([P, P], F32)
         make_identity(nc, ident[:])
-        eps_col = keep.tile([P, 1], F32)
-        nc.vector.memset(eps_col[:], EPS)
 
         ln_cols_ps = psum.tile([P, P], BF16, tag="bank")
         nc.tensor.transpose(ln_cols_ps[:], ln_rows[:], ident_bf[:])
@@ -84,7 +99,8 @@ def tile_stulayer_pa_kernel(tc, src, ln1_w, ln1_b, w_uvqk, b_uvqk, out):
         nc.vector.tensor_copy(out=gain_shift[:], in_=ln_cols_ps[:, 0 : 2 * GROUPS])
 
         bias_all = keep.tile([P, N], BF16)
-        for pair in range(BIAS_ROWS // 2):
+
+        def spread_bias(pair):
             bias_ps = psum.tile([P, 2 * N_TILE], BF16, tag="bank")
             for half in range(2):
                 r = 2 * pair + half
@@ -101,7 +117,12 @@ def tile_stulayer_pa_kernel(tc, src, ln1_w, ln1_b, w_uvqk, b_uvqk, out):
 
         stats = keep.tile([P, TOKEN_TILES, D // BN_FMAX, BN_STATS_DIM], F32)
         mean_var = keep.tile([P, TOKEN_TILES, BN_AGGR_DIM], F32)
-        for i in range(TOKEN_TILES):
+        std = keep.tile([P, TOKEN_TILES], F32)
+        rstd = keep.tile([P, TOKEN_TILES], F32)
+        neg_mean = keep.tile([P, TOKEN_TILES], F32)
+        xhat_tiles = []
+
+        def statistics(i):
             for h in range(D // BN_FMAX):
                 nc.vector.bn_stats(
                     out=stats[:, i, h, :], in_=x_tiles[i][:, h * BN_FMAX : (h + 1) * BN_FMAX]
@@ -109,21 +130,19 @@ def tile_stulayer_pa_kernel(tc, src, ln1_w, ln1_b, w_uvqk, b_uvqk, out):
             nc.vector.bn_aggr(
                 out=mean_var[:, i, :], in_=stats[:, i, :, :].rearrange("p h s -> p (h s)")
             )
-        std = keep.tile([P, TOKEN_TILES], F32)
-        nc.scalar.activation(
-            out=std[:], in_=mean_var[:, :, 1], func=ACT.Sqrt, bias=eps_col[:, 0:1], scale=1.0
-        )
-        rstd = keep.tile([P, TOKEN_TILES], F32)
-        nc.vector.reciprocal(out=rstd[:], in_=std[:])
-        neg_mean = keep.tile([P, TOKEN_TILES], F32)
-        nc.vector.tensor_scalar(
-            out=neg_mean[:], in0=mean_var[:, :, 0], scalar1=-1.0, scalar2=None, op0=ALU.mult
-        )
+            nc.scalar.activation(
+                out=std[:, i : i + 1], in_=mean_var[:, i, 1:2], func=ACT.Sqrt,
+                bias=eps_col[:, 0:1], scale=1.0,
+            )
 
-        xhat_tiles = []
-        for i in range(TOKEN_TILES):
+        def normalise(i):
+            nc.vector.reciprocal(out=rstd[:, i : i + 1], in_=std[:, i : i + 1])
+            nc.vector.tensor_scalar(
+                out=neg_mean[:, i : i + 1], in0=mean_var[:, i, 0:1], scalar1=-1.0, scalar2=None,
+                op0=ALU.mult,
+            )
             xhat_i = keep.tile([P, D], F32, name="xhat%d" % i)
-            engine = nc.vector if i % 2 == 0 else nc.gpsimd
+            engine = nc.vector if i == TOKEN_TILES - 1 else nc.gpsimd
             engine.tensor_scalar(
                 out=xhat_i[:],
                 in0=x_tiles[i][:],
@@ -134,24 +153,115 @@ def tile_stulayer_pa_kernel(tc, src, ln1_w, ln1_b, w_uvqk, b_uvqk, out):
             )
             xhat_tiles.append(xhat_i)
 
+        pairs_per_tile = PARTS // 2 // TOKEN_TILES
+        for i in range(TOKEN_TILES):
+            for pair in range(i * pairs_per_tile, (i + 1) * pairs_per_tile):
+                spread_bias(pair)
+            statistics(i)
+            if i >= 1:
+                normalise(i - 1)
+        normalise(TOKEN_TILES - 1)
+
+        xt_banks = []
+        for g in range(GROUPS):
+            xt_g = psum.tile([P, T], F32, name="xt%d" % g, tag="bank")
+            xt_banks.append(xt_g)
+        for i in range(TOKEN_TILES):
+            for g in range(GROUPS):
+                nc.tensor.transpose(
+                    xt_banks[g][:, i * P : (i + 1) * P],
+                    xhat_tiles[i][:, g * P : (g + 1) * P],
+                    ident[:],
+                )
+
+        grouped = {}
+        codes = {}
+        accs = {}
+        stages = {}
+
+        def regroup_unit(part, c):
+            chunk = part // PARTS_PER_CHUNK
+            first = (part % PARTS_PER_CHUNK) * N_TILE
+            w_grouped = grouped_pool.tile([P, N_TILE, PACK], BF16, align_bytes=64)
+            if c == PASSES - 1 and part % VECTOR_EVERY == VECTOR_EVERY - 1:
+                copy = nc.vector.tensor_copy
+            else:
+                copy = nc.scalar.copy
+            regroup(copy, w_grouped[:], raw[(chunk, c)][:, :, first : first + N_TILE])
+            grouped[(part, c)] = w_grouped
+
+        def quantise_unit(part, c):
+            w_codes = code_pool.tile([P, N_TILE], U32, align_bytes=64)
+            w_scales = code_pool.tile([P, N_TILE], U8, align_bytes=64)
+            nc.vector.quantize_mx(
+                out=w_codes[:].bitcast(FP8X4),
+                scales=w_scales[:],
+                in_=grouped[(part, c)][:].rearrange("p n t -> p (n t)"),
+            )
+            codes[(part, c)] = (w_codes, w_scales)
+
+        def multiply(part):
+            for i in range(TOKEN_TILES):
+                acc_i = psum.tile([P, N_TILE], F32, name="acc_i", tag="bank")
+                accs[(part, i)] = acc_i
+            for c in range(PASSES):
+                w_codes, w_scales = codes[(part, c)]
+                for i in range(TOKEN_TILES):
+                    tokens = slice(c * T + i * P, c * T + (i + 1) * P)
+                    nc.tensor.matmul_mx(
+                        out=accs[(part, i)][:],
+                        lhsT=x_codes[:, tokens].bitcast(FP8X4),
+                        lhsT_scale=x_scales[:, tokens],
+                        rhs=w_codes[:].bitcast(FP8X4),
+                        rhs_scale=w_scales[:],
+                        start=(c == 0),
+                        stop=(c == PASSES - 1),
+                    )
+
+        def add_bias_and_store(part):
+            chunk = part // PARTS_PER_CHUNK
+            local = (part % PARTS_PER_CHUNK) * N_TILE
+            first = part * N_TILE
+            for i in range(TOKEN_TILES):
+                if local == 0:
+                    stage_i = stage_pool.tile([P, LOAD_COLS], F32, name="stage_i", tag="stage")
+                    stages[(chunk, i)] = stage_i
+                stage = stages[(chunk, i)]
+                token_rows = slice(i * P, (i + 1) * P)
+                nc.vector.tensor_tensor(
+                    out=stage[:, local : local + N_TILE],
+                    in0=accs[(part, i)][:],
+                    in1=bias_all[:, first : first + N_TILE],
+                    op=ALU.add,
+                )
+                if chunk == CHUNKS - 1:
+                    nc.sync.dma_start(
+                        out=out_rows[token_rows, first : first + N_TILE],
+                        in_=stage[:, local : local + N_TILE],
+                    )
+                elif local + N_TILE == LOAD_COLS:
+                    nc.sync.dma_start(
+                        out=out_rows[token_rows, chunk * LOAD_COLS : (chunk + 1) * LOAD_COLS],
+                        in_=stage[:],
+                    )
+
+        regroup_unit(0, 0)
+
         x_norm = keep.tile([P, GROUPS, T], BF16)
         for g in range(GROUPS):
-            xt = psum.tile([P, T], F32, tag="bank")
-            for i in range(TOKEN_TILES):
-                nc.tensor.transpose(
-                    xt[:, i * P : (i + 1) * P], xhat_tiles[i][:, g * P : (g + 1) * P], ident[:]
-                )
             gain = gain_shift[:, g : g + 1]
             shift = gain_shift[:, GROUPS + g : GROUPS + g + 1]
             if g % 2 == 0:
                 nc.scalar.activation(
-                    out=x_norm[:, g, :], in_=xt[:], func=ACT.Identity, scale=gain, bias=shift
+                    out=x_norm[:, g, :], in_=xt_banks[g][:], func=ACT.Identity,
+                    scale=gain, bias=shift,
                 )
             else:
                 nc.vector.tensor_scalar(
-                    out=x_norm[:, g, :], in0=xt[:], scalar1=gain, scalar2=shift,
+                    out=x_norm[:, g, :], in0=xt_banks[g][:], scalar1=gain, scalar2=shift,
                     op0=ALU.mult, op1=ALU.add,
                 )
+        regroup_unit(0, 1)
 
         x_grouped = keep.tile([P, PASSES, T, PACK], BF16, align_bytes=64)
         for c in range(PASSES):
@@ -168,63 +278,16 @@ def tile_stulayer_pa_kernel(tc, src, ln1_w, ln1_b, w_uvqk, b_uvqk, out):
             in_=x_grouped[:].rearrange("p c n t -> p (c n t)"),
         )
 
-        for chunk in range(N // LOAD_COLS):
-            chunk_cols = slice(chunk * LOAD_COLS, (chunk + 1) * LOAD_COLS)
-            raw = []
-            for c in range(PASSES):
-                raw_c = raw_pool.tile([P, PACK, LOAD_COLS], BF16, name="raw_c", tag="raw")
-                nc.sync.dma_start(out=raw_c[:], in_=w_view[:, c, :, chunk_cols])
-                raw.append(raw_c)
-            stages = []
-            for i in range(TOKEN_TILES):
-                stage_i = stage_pool.tile([P, LOAD_COLS], F32, name="stage_i", tag="stage")
-                stages.append(stage_i)
-
-            for part in range(LOAD_COLS // N_TILE):
-                local = slice(part * N_TILE, (part + 1) * N_TILE)
-                first = chunk * LOAD_COLS + part * N_TILE
-                accs = []
-                for i in range(TOKEN_TILES):
-                    acc_i = psum.tile([P, N_TILE], F32, name="acc_i", tag="bank")
-                    accs.append(acc_i)
+        for part in range(PARTS + 1):
+            if 1 <= part < PARTS:
                 for c in range(PASSES):
-                    w_grouped = grouped_pool.tile([P, N_TILE, PACK], BF16, align_bytes=64)
-                    if c == PASSES - 1 and (first // N_TILE) % VECTOR_EVERY == VECTOR_EVERY - 1:
-                        regroup(nc.vector.tensor_copy, w_grouped[:], raw[c][:, :, local])
-                    else:
-                        regroup(nc.scalar.copy, w_grouped[:], raw[c][:, :, local])
-                    w_codes = code_pool.tile([P, N_TILE], U32, align_bytes=64)
-                    w_scales = code_pool.tile([P, N_TILE], U8, align_bytes=64)
-                    nc.vector.quantize_mx(
-                        out=w_codes[:].bitcast(FP8X4),
-                        scales=w_scales[:],
-                        in_=w_grouped[:].rearrange("p n t -> p (n t)"),
-                    )
-                    for i in range(TOKEN_TILES):
-                        tokens = slice(c * T + i * P, c * T + (i + 1) * P)
-                        nc.tensor.matmul_mx(
-                            out=accs[i][:],
-                            lhsT=x_codes[:, tokens].bitcast(FP8X4),
-                            lhsT_scale=x_scales[:, tokens],
-                            rhs=w_codes[:].bitcast(FP8X4),
-                            rhs_scale=w_scales[:],
-                            start=(c == 0),
-                            stop=(c == PASSES - 1),
-                        )
-                for i in range(TOKEN_TILES):
-                    nc.vector.tensor_tensor(
-                        out=stages[i][:, local],
-                        in0=accs[i][:],
-                        in1=bias_all[:, first : first + N_TILE],
-                        op=ALU.add,
-                    )
-                    if chunk == LAST_CHUNK:
-                        nc.sync.dma_start(
-                            out=out_rows[i * P : (i + 1) * P, first : first + N_TILE],
-                            in_=stages[i][:, local],
-                        )
-            if chunk != LAST_CHUNK:
-                for i in range(TOKEN_TILES):
-                    nc.sync.dma_start(
-                        out=out_rows[i * P : (i + 1) * P, chunk_cols], in_=stages[i][:]
-                    )
+                    regroup_unit(part, c)
+            if part < PARTS:
+                chunk = part // PARTS_PER_CHUNK
+                if part % PARTS_PER_CHUNK == PARTS_PER_CHUNK - 1 and chunk + CHUNKS_AHEAD < CHUNKS:
+                    load_chunk(chunk + CHUNKS_AHEAD)
+                for c in range(PASSES):
+                    quantise_unit(part, c)
+                multiply(part)
+            if part >= 1:
+                add_bias_and_store(part - 1)

@@ -27,7 +27,7 @@ CHUNKS = N // LOAD_COLS
 PARTS_PER_CHUNK = LOAD_COLS // N_TILE
 CHUNKS_AHEAD = 5
 RUN = 4
-VECTOR_EVERY = 4
+GPSIMD_EVERY = 2
 BN_FMAX = 512
 BN_STATS_DIM = 6
 BN_AGGR_DIM = 2
@@ -52,6 +52,7 @@ def tile_stulayer_pa_kernel(tc, src, ln1_w, ln1_b, w_uvqk, b_uvqk, out):
         keep = ctx.enter_context(tc.tile_pool(name="keep", bufs=1))
         raw_pool = ctx.enter_context(tc.tile_pool(name="raw", bufs=CHUNKS_AHEAD * PASSES))
         grouped_pool = ctx.enter_context(tc.tile_pool(name="grouped", bufs=6))
+        gpsimd_pool = ctx.enter_context(tc.tile_pool(name="gpsimd_grouped", bufs=1))
         code_pool = ctx.enter_context(tc.tile_pool(name="codes", bufs=8))
         stage_pool = ctx.enter_context(tc.tile_pool(name="stage", bufs=2 * TOKEN_TILES))
         psum = ctx.enter_context(tc.psum_pool(name="psum", bufs=8))
@@ -155,9 +156,9 @@ def tile_stulayer_pa_kernel(tc, src, ln1_w, ln1_b, w_uvqk, b_uvqk, out):
 
         pairs_per_tile = PARTS // 2 // TOKEN_TILES
         for i in range(TOKEN_TILES):
+            statistics(i)
             for pair in range(i * pairs_per_tile, (i + 1) * pairs_per_tile):
                 spread_bias(pair)
-            statistics(i)
             if i >= 1:
                 normalise(i - 1)
         normalise(TOKEN_TILES - 1)
@@ -179,15 +180,21 @@ def tile_stulayer_pa_kernel(tc, src, ln1_w, ln1_b, w_uvqk, b_uvqk, out):
         accs = {}
         stages = {}
 
+        def gpsimd_copy(out, in_):
+            nc.gpsimd.tensor_scalar(
+                out=out, in0=in_, scalar1=1.0, scalar2=0.0, op0=ALU.mult, op1=ALU.add
+            )
+
         def regroup_unit(part, c):
             chunk = part // PARTS_PER_CHUNK
             first = (part % PARTS_PER_CHUNK) * N_TILE
-            w_grouped = grouped_pool.tile([P, N_TILE, PACK], BF16, align_bytes=64)
-            if c == PASSES - 1 and part % VECTOR_EVERY == VECTOR_EVERY - 1:
-                copy = nc.vector.tensor_copy
+            rows = raw[(chunk, c)][:, :, first : first + N_TILE]
+            if c == PASSES - 1 and part % GPSIMD_EVERY == GPSIMD_EVERY - 1:
+                w_grouped = gpsimd_pool.tile([P, N_TILE, PACK], BF16, align_bytes=64)
+                regroup(gpsimd_copy, w_grouped[:], rows)
             else:
-                copy = nc.scalar.copy
-            regroup(copy, w_grouped[:], raw[(chunk, c)][:, :, first : first + N_TILE])
+                w_grouped = grouped_pool.tile([P, N_TILE, PACK], BF16, align_bytes=64)
+                regroup(nc.scalar.copy, w_grouped[:], rows)
             grouped[(part, c)] = w_grouped
 
         def quantise_unit(part, c):
@@ -246,6 +253,7 @@ def tile_stulayer_pa_kernel(tc, src, ln1_w, ln1_b, w_uvqk, b_uvqk, out):
                     )
 
         regroup_unit(0, 0)
+        quantise_unit(0, 0)
 
         x_norm = keep.tile([P, GROUPS, T], BF16)
         for g in range(GROUPS):
@@ -287,7 +295,8 @@ def tile_stulayer_pa_kernel(tc, src, ln1_w, ln1_b, w_uvqk, b_uvqk, out):
                 if part % PARTS_PER_CHUNK == PARTS_PER_CHUNK - 1 and chunk + CHUNKS_AHEAD < CHUNKS:
                     load_chunk(chunk + CHUNKS_AHEAD)
                 for c in range(PASSES):
-                    quantise_unit(part, c)
+                    if (part, c) not in codes:
+                        quantise_unit(part, c)
                 multiply(part)
             if part >= 1:
                 add_bias_and_store(part - 1)

@@ -22,10 +22,13 @@ GROUPS = PASSES * PACK
 TOKEN_TILES = T // P
 N_TILE = 512
 PARTS = N // N_TILE
-LOAD_COLS = 1024
-CHUNKS = N // LOAD_COLS
-PARTS_PER_CHUNK = LOAD_COLS // N_TILE
-CHUNKS_AHEAD = 5
+LOAD_COLS = 2048
+PARTS_PER_LOAD = LOAD_COLS // N_TILE
+LOADS = (N // LOAD_COLS) * PASSES
+LOADS_AHEAD = 6
+STORE_COLS = 1024
+STORES = N // STORE_COLS
+PARTS_PER_STORE = STORE_COLS // N_TILE
 RUN = 4
 GPSIMD_EVERY = 2
 BN_FMAX = 512
@@ -50,253 +53,263 @@ def tile_stulayer_pa_kernel(tc, src, ln1_w, ln1_b, w_uvqk, b_uvqk, out):
 
     with ExitStack() as ctx:
         keep = ctx.enter_context(tc.tile_pool(name="keep", bufs=1))
-        raw_pool = ctx.enter_context(tc.tile_pool(name="raw", bufs=CHUNKS_AHEAD * PASSES))
-        grouped_pool = ctx.enter_context(tc.tile_pool(name="grouped", bufs=6))
-        gpsimd_pool = ctx.enter_context(tc.tile_pool(name="gpsimd_grouped", bufs=1))
-        code_pool = ctx.enter_context(tc.tile_pool(name="codes", bufs=8))
-        stage_pool = ctx.enter_context(tc.tile_pool(name="stage", bufs=2 * TOKEN_TILES))
+        raw_pool = ctx.enter_context(tc.tile_pool(name="raw", bufs=LOADS_AHEAD))
+        grouped_pool = ctx.enter_context(tc.tile_pool(name="grouped", bufs=3))
+        code_pool = ctx.enter_context(tc.tile_pool(name="codes", bufs=4))
         psum = ctx.enter_context(tc.psum_pool(name="psum", bufs=8))
         ctx.enter_context(tc.manual_schedule())
 
-        raw = {}
+        raw = []
 
-        def load_chunk(chunk):
-            for c in range(PASSES):
-                raw_c = raw_pool.tile([P, PACK, LOAD_COLS], BF16, name="raw_c", tag="raw")
-                nc.sync.dma_start(
-                    out=raw_c[:], in_=w_view[:, c, :, chunk * LOAD_COLS : (chunk + 1) * LOAD_COLS]
-                )
-                raw[(chunk, c)] = raw_c
-
-        ln_rows = keep.tile([P, P], BF16)
-        nc.vector.memset(ln_rows[:], 0.0)
-        bias_rows = keep.tile([P, N_TILE], BF16)
-        nc.vector.memset(bias_rows[:], 0.0)
-        eps_col = keep.tile([P, 1], F32)
-        nc.vector.memset(eps_col[:], EPS)
-        nc.sync.dma_start(
-            out=bias_rows[0:PARTS, :], in_=b_uvqk.rearrange("(r n) -> r n", n=N_TILE)
-        )
-        nc.sync.dma_start(out=ln_rows[0:GROUPS, :], in_=ln1_w.rearrange("(g p) -> g p", p=P))
-        nc.sync.dma_start(
-            out=ln_rows[GROUPS : 2 * GROUPS, :], in_=ln1_b.rearrange("(g p) -> g p", p=P)
-        )
-        x_tiles = []
-        for i in range(TOKEN_TILES):
-            x_i = keep.tile([P, D], BF16, name="x%d" % i)
-            nc.sync.dma_start(out=x_i[:], in_=src_rows[i * P : (i + 1) * P, :])
-            x_tiles.append(x_i)
-        for chunk in range(CHUNKS_AHEAD):
-            load_chunk(chunk)
-
-        ident_bf = keep.tile([P, P], BF16)
-        make_identity(nc, ident_bf[:])
-        ident = keep.tile([P, P], F32)
-        make_identity(nc, ident[:])
-
-        ln_cols_ps = psum.tile([P, P], BF16, tag="bank")
-        nc.tensor.transpose(ln_cols_ps[:], ln_rows[:], ident_bf[:])
-        gain_shift = keep.tile([P, 2 * GROUPS], F32)
-        nc.vector.tensor_copy(out=gain_shift[:], in_=ln_cols_ps[:, 0 : 2 * GROUPS])
-
-        bias_all = keep.tile([P, N], BF16)
-
-        def spread_bias(pair):
-            bias_ps = psum.tile([P, 2 * N_TILE], BF16, tag="bank")
-            for half in range(2):
-                r = 2 * pair + half
-                nc.tensor.matmul(
-                    out=bias_ps[:, half * N_TILE : (half + 1) * N_TILE],
-                    lhsT=ident_bf[:, r : r + 1].to_broadcast([P, P]),
-                    rhs=bias_rows[:],
-                    start=True,
-                    stop=True,
-                )
-            nc.scalar.copy(
-                out=bias_all[:, pair * 2 * N_TILE : (pair + 1) * 2 * N_TILE], in_=bias_ps[:]
+        def load_w(number, piece, pieces):
+            if piece == 0:
+                raw_tile = raw_pool.tile([P, PACK, LOAD_COLS], BF16, name="raw_tile", tag="raw")
+                raw.append(raw_tile)
+            width = LOAD_COLS // pieces
+            local = piece * width
+            first = (number // PASSES) * LOAD_COLS + local
+            nc.sync.dma_start(
+                out=raw[number][:, :, local : local + width],
+                in_=w_view[:, number % PASSES, :, first : first + width],
             )
 
-        stats = keep.tile([P, TOKEN_TILES, D // BN_FMAX, BN_STATS_DIM], F32)
-        mean_var = keep.tile([P, TOKEN_TILES, BN_AGGR_DIM], F32)
-        std = keep.tile([P, TOKEN_TILES], F32)
-        rstd = keep.tile([P, TOKEN_TILES], F32)
-        neg_mean = keep.tile([P, TOKEN_TILES], F32)
-        xhat_tiles = []
+        with tc.tile_pool(name="head", bufs=1) as head:
 
-        def statistics(i):
-            for h in range(D // BN_FMAX):
-                nc.vector.bn_stats(
-                    out=stats[:, i, h, :], in_=x_tiles[i][:, h * BN_FMAX : (h + 1) * BN_FMAX]
-                )
-            nc.vector.bn_aggr(
-                out=mean_var[:, i, :], in_=stats[:, i, :, :].rearrange("p h s -> p (h s)")
-            )
-            nc.scalar.activation(
-                out=std[:, i : i + 1], in_=mean_var[:, i, 1:2], func=ACT.Sqrt,
-                bias=eps_col[:, 0:1], scale=1.0,
-            )
-
-        def normalise(i):
-            nc.vector.reciprocal(out=rstd[:, i : i + 1], in_=std[:, i : i + 1])
-            nc.vector.tensor_scalar(
-                out=neg_mean[:, i : i + 1], in0=mean_var[:, i, 0:1], scalar1=-1.0, scalar2=None,
-                op0=ALU.mult,
-            )
-            xhat_i = keep.tile([P, D], F32, name="xhat%d" % i)
-            engine = nc.vector if i == TOKEN_TILES - 1 else nc.gpsimd
-            engine.tensor_scalar(
-                out=xhat_i[:],
-                in0=x_tiles[i][:],
-                scalar1=neg_mean[:, i : i + 1],
-                scalar2=rstd[:, i : i + 1],
-                op0=ALU.add,
-                op1=ALU.mult,
-            )
-            xhat_tiles.append(xhat_i)
-
-        pairs_per_tile = PARTS // 2 // TOKEN_TILES
-        for i in range(TOKEN_TILES):
-            statistics(i)
-            for pair in range(i * pairs_per_tile, (i + 1) * pairs_per_tile):
-                spread_bias(pair)
-            if i >= 1:
-                normalise(i - 1)
-        normalise(TOKEN_TILES - 1)
-
-        xt_banks = []
-        for g in range(GROUPS):
-            xt_g = psum.tile([P, T], F32, name="xt%d" % g, tag="bank")
-            xt_banks.append(xt_g)
-        for i in range(TOKEN_TILES):
-            for g in range(GROUPS):
-                nc.tensor.transpose(
-                    xt_banks[g][:, i * P : (i + 1) * P],
-                    xhat_tiles[i][:, g * P : (g + 1) * P],
-                    ident[:],
-                )
-
-        grouped = {}
-        codes = {}
-        accs = {}
-        stages = {}
-
-        def gpsimd_copy(out, in_):
-            nc.gpsimd.tensor_scalar(
-                out=out, in0=in_, scalar1=1.0, scalar2=0.0, op0=ALU.mult, op1=ALU.add
-            )
-
-        def regroup_unit(part, c):
-            chunk = part // PARTS_PER_CHUNK
-            first = (part % PARTS_PER_CHUNK) * N_TILE
-            rows = raw[(chunk, c)][:, :, first : first + N_TILE]
-            if c == PASSES - 1 and part % GPSIMD_EVERY == GPSIMD_EVERY - 1:
-                w_grouped = gpsimd_pool.tile([P, N_TILE, PACK], BF16, align_bytes=64)
-                regroup(gpsimd_copy, w_grouped[:], rows)
-            else:
-                w_grouped = grouped_pool.tile([P, N_TILE, PACK], BF16, align_bytes=64)
-                regroup(nc.scalar.copy, w_grouped[:], rows)
-            grouped[(part, c)] = w_grouped
-
-        def quantise_unit(part, c):
-            w_codes = code_pool.tile([P, N_TILE], U32, align_bytes=64)
-            w_scales = code_pool.tile([P, N_TILE], U8, align_bytes=64)
-            nc.vector.quantize_mx(
-                out=w_codes[:].bitcast(FP8X4),
-                scales=w_scales[:],
-                in_=grouped[(part, c)][:].rearrange("p n t -> p (n t)"),
-            )
-            codes[(part, c)] = (w_codes, w_scales)
-
-        def multiply(part):
+            ln_rows = keep.tile([P, P], BF16)
+            nc.vector.memset(ln_rows[:], 0.0)
+            bias_rows = keep.tile([P, N_TILE], BF16)
+            nc.vector.memset(bias_rows[:], 0.0)
+            eps_col = keep.tile([P, 1], F32)
+            nc.vector.memset(eps_col[:], EPS)
+            x_tiles = []
             for i in range(TOKEN_TILES):
-                acc_i = psum.tile([P, N_TILE], F32, name="acc_i", tag="bank")
-                accs[(part, i)] = acc_i
-            for c in range(PASSES):
-                w_codes, w_scales = codes[(part, c)]
-                for i in range(TOKEN_TILES):
-                    tokens = slice(c * T + i * P, c * T + (i + 1) * P)
-                    nc.tensor.matmul_mx(
-                        out=accs[(part, i)][:],
-                        lhsT=x_codes[:, tokens].bitcast(FP8X4),
-                        lhsT_scale=x_scales[:, tokens],
-                        rhs=w_codes[:].bitcast(FP8X4),
-                        rhs_scale=w_scales[:],
-                        start=(c == 0),
-                        stop=(c == PASSES - 1),
+                x_i = head.tile([P, D], BF16, name="x%d" % i)
+                nc.sync.dma_start(out=x_i[:], in_=src_rows[i * P : (i + 1) * P, :])
+                x_tiles.append(x_i)
+                if i == 0:
+                    nc.sync.dma_start(
+                        out=bias_rows[0:PARTS, :], in_=b_uvqk.rearrange("(r n) -> r n", n=N_TILE)
                     )
+                    nc.sync.dma_start(
+                        out=ln_rows[0:GROUPS, :], in_=ln1_w.rearrange("(g p) -> g p", p=P)
+                    )
+                    nc.sync.dma_start(
+                        out=ln_rows[GROUPS : 2 * GROUPS, :], in_=ln1_b.rearrange("(g p) -> g p", p=P)
+                    )
+            for piece in range(2):
+                for number in range(PASSES):
+                    load_w(number, piece, 2)
+            for number in range(PASSES, LOADS_AHEAD):
+                load_w(number, 0, 1)
 
-        def add_bias_and_store(part):
-            chunk = part // PARTS_PER_CHUNK
-            local = (part % PARTS_PER_CHUNK) * N_TILE
-            first = part * N_TILE
-            for i in range(TOKEN_TILES):
-                if local == 0:
-                    stage_i = stage_pool.tile([P, LOAD_COLS], F32, name="stage_i", tag="stage")
-                    stages[(chunk, i)] = stage_i
-                stage = stages[(chunk, i)]
-                token_rows = slice(i * P, (i + 1) * P)
-                nc.vector.tensor_tensor(
-                    out=stage[:, local : local + N_TILE],
-                    in0=accs[(part, i)][:],
-                    in1=bias_all[:, first : first + N_TILE],
-                    op=ALU.add,
+
+            ident_bf = keep.tile([P, P], BF16)
+            make_identity(nc, ident_bf[:])
+            ident = keep.tile([P, P], F32)
+            make_identity(nc, ident[:])
+
+            ln_cols_ps = psum.tile([P, P], BF16, tag="bank")
+            nc.tensor.transpose(ln_cols_ps[:], ln_rows[:], ident_bf[:])
+            gain_shift = keep.tile([P, 2 * GROUPS], F32)
+            nc.vector.tensor_copy(out=gain_shift[:], in_=ln_cols_ps[:, 0 : 2 * GROUPS])
+
+            bias_all = keep.tile([P, N], BF16)
+
+            def spread_bias(pair):
+                bias_ps = psum.tile([P, 2 * N_TILE], BF16, tag="bank")
+                for half in range(2):
+                    r = 2 * pair + half
+                    nc.tensor.matmul(
+                        out=bias_ps[:, half * N_TILE : (half + 1) * N_TILE],
+                        lhsT=ident_bf[:, r : r + 1].to_broadcast([P, P]),
+                        rhs=bias_rows[:],
+                        start=True,
+                        stop=True,
+                    )
+                nc.scalar.copy(
+                    out=bias_all[:, pair * 2 * N_TILE : (pair + 1) * 2 * N_TILE], in_=bias_ps[:]
                 )
-                if chunk == CHUNKS - 1:
-                    nc.sync.dma_start(
-                        out=out_rows[token_rows, first : first + N_TILE],
-                        in_=stage[:, local : local + N_TILE],
-                    )
-                elif local + N_TILE == LOAD_COLS:
-                    nc.sync.dma_start(
-                        out=out_rows[token_rows, chunk * LOAD_COLS : (chunk + 1) * LOAD_COLS],
-                        in_=stage[:],
-                    )
 
-        regroup_unit(0, 0)
-        quantise_unit(0, 0)
+            stats = keep.tile([P, TOKEN_TILES, D // BN_FMAX, BN_STATS_DIM], F32)
+            mean_var = keep.tile([P, TOKEN_TILES, BN_AGGR_DIM], F32)
+            std = keep.tile([P, TOKEN_TILES], F32)
+            rstd = keep.tile([P, TOKEN_TILES], F32)
+            neg_mean = keep.tile([P, TOKEN_TILES], F32)
+            xhat_tiles = []
 
-        x_norm = keep.tile([P, GROUPS, T], BF16)
-        for g in range(GROUPS):
-            gain = gain_shift[:, g : g + 1]
-            shift = gain_shift[:, GROUPS + g : GROUPS + g + 1]
-            if g % 2 == 0:
+            def statistics(i):
+                for h in range(D // BN_FMAX):
+                    nc.vector.bn_stats(
+                        out=stats[:, i, h, :], in_=x_tiles[i][:, h * BN_FMAX : (h + 1) * BN_FMAX]
+                    )
+                nc.vector.bn_aggr(
+                    out=mean_var[:, i, :], in_=stats[:, i, :, :].rearrange("p h s -> p (h s)")
+                )
                 nc.scalar.activation(
-                    out=x_norm[:, g, :], in_=xt_banks[g][:], func=ACT.Identity,
-                    scale=gain, bias=shift,
+                    out=std[:, i : i + 1], in_=mean_var[:, i, 1:2], func=ACT.Sqrt,
+                    bias=eps_col[:, 0:1], scale=1.0,
                 )
-            else:
-                nc.vector.tensor_scalar(
-                    out=x_norm[:, g, :], in0=xt_banks[g][:], scalar1=gain, scalar2=shift,
-                    op0=ALU.mult, op1=ALU.add,
-                )
-        regroup_unit(0, 1)
 
-        x_grouped = keep.tile([P, PASSES, T, PACK], BF16, align_bytes=64)
-        for c in range(PASSES):
-            regroup(
-                nc.vector.tensor_copy,
-                x_grouped[:, c, :, :],
-                x_norm[:, c * PACK : (c + 1) * PACK, :],
+            def normalise(i):
+                nc.vector.reciprocal(out=rstd[:, i : i + 1], in_=std[:, i : i + 1])
+                nc.vector.tensor_scalar(
+                    out=neg_mean[:, i : i + 1], in0=mean_var[:, i, 0:1], scalar1=-1.0, scalar2=None,
+                    op0=ALU.mult,
+                )
+                xhat_i = head.tile([P, D], F32, name="xhat%d" % i)
+                engine = nc.vector if i == TOKEN_TILES - 1 else nc.gpsimd
+                engine.tensor_scalar(
+                    out=xhat_i[:],
+                    in0=x_tiles[i][:],
+                    scalar1=neg_mean[:, i : i + 1],
+                    scalar2=rstd[:, i : i + 1],
+                    op0=ALU.add,
+                    op1=ALU.mult,
+                )
+                xhat_tiles.append(xhat_i)
+
+            pairs_per_tile = PARTS // 2 // TOKEN_TILES
+            for i in range(TOKEN_TILES):
+                statistics(i)
+                for pair in range(i * pairs_per_tile, (i + 1) * pairs_per_tile):
+                    spread_bias(pair)
+                if i >= 1:
+                    normalise(i - 1)
+            normalise(TOKEN_TILES - 1)
+
+            xt_banks = []
+            for g in range(GROUPS):
+                xt_g = psum.tile([P, T], F32, name="xt%d" % g, tag="bank")
+                xt_banks.append(xt_g)
+            for i in range(TOKEN_TILES):
+                for g in range(GROUPS):
+                    nc.tensor.transpose(
+                        xt_banks[g][:, i * P : (i + 1) * P],
+                        xhat_tiles[i][:, g * P : (g + 1) * P],
+                        ident[:],
+                    )
+
+            grouped = {}
+            codes = {}
+            accs = {}
+            stages = {}
+
+            def gpsimd_copy(out, in_):
+                nc.gpsimd.tensor_scalar(
+                    out=out, in0=in_, scalar1=1.0, scalar2=0.0, op0=ALU.mult, op1=ALU.add
+                )
+
+            def regroup_part(part):
+                w_grouped = grouped_pool.tile([P, PASSES, N_TILE, PACK], BF16, align_bytes=64)
+                first = (part % PARTS_PER_LOAD) * N_TILE
+                for c in range(PASSES):
+                    number = (part // PARTS_PER_LOAD) * PASSES + c
+                    if c == PASSES - 1 and part % GPSIMD_EVERY == 0:
+                        copy = gpsimd_copy
+                    else:
+                        copy = nc.scalar.copy
+                    regroup(copy, w_grouped[:, c, :, :], raw[number][:, :, first : first + N_TILE])
+                grouped[part] = w_grouped
+
+            def quantise_part(part):
+                w_codes = code_pool.tile([P, PASSES * N_TILE], U32, align_bytes=64)
+                w_scales = code_pool.tile([P, PASSES * N_TILE], U8, align_bytes=64)
+                nc.vector.quantize_mx(
+                    out=w_codes[:].bitcast(FP8X4),
+                    scales=w_scales[:],
+                    in_=grouped[part][:].rearrange("p c n t -> p (c n t)"),
+                )
+                codes[part] = (w_codes, w_scales)
+
+            def multiply(part):
+                for i in range(TOKEN_TILES):
+                    acc_i = psum.tile([P, N_TILE], F32, name="acc_i", tag="bank")
+                    accs[(part, i)] = acc_i
+                w_codes, w_scales = codes[part]
+                for c in range(PASSES):
+                    columns = slice(c * N_TILE, (c + 1) * N_TILE)
+                    for i in range(TOKEN_TILES):
+                        tokens = slice(c * T + i * P, c * T + (i + 1) * P)
+                        nc.tensor.matmul_mx(
+                            out=accs[(part, i)][:],
+                            lhsT=x_codes[:, tokens].bitcast(FP8X4),
+                            lhsT_scale=x_scales[:, tokens],
+                            rhs=w_codes[:, columns].bitcast(FP8X4),
+                            rhs_scale=w_scales[:, columns],
+                            start=(c == 0),
+                            stop=(c == PASSES - 1),
+                        )
+
+            def add_bias_and_store(part):
+                store = part // PARTS_PER_STORE
+                local = (part % PARTS_PER_STORE) * N_TILE
+                first = part * N_TILE
+                for i in range(TOKEN_TILES):
+                    if local == 0:
+                        stage_i = stage_pool.tile([P, STORE_COLS], F32, name="stage_i", tag="stage")
+                        stages[(store, i)] = stage_i
+                    stage = stages[(store, i)]
+                    token_rows = slice(i * P, (i + 1) * P)
+                    nc.vector.tensor_tensor(
+                        out=stage[:, local : local + N_TILE],
+                        in0=accs[(part, i)][:],
+                        in1=bias_all[:, first : first + N_TILE],
+                        op=ALU.add,
+                    )
+                    if store == STORES - 1:
+                        nc.sync.dma_start(
+                            out=out_rows[token_rows, first : first + N_TILE],
+                            in_=stage[:, local : local + N_TILE],
+                        )
+                    elif local + N_TILE == STORE_COLS:
+                        nc.sync.dma_start(
+                            out=out_rows[token_rows, store * STORE_COLS : (store + 1) * STORE_COLS],
+                            in_=stage[:],
+                        )
+
+            regroup_part(0)
+
+            x_norm = head.tile([P, GROUPS, T], BF16)
+            for g in range(GROUPS):
+                gain = gain_shift[:, g : g + 1]
+                shift = gain_shift[:, GROUPS + g : GROUPS + g + 1]
+                if g % 2 == 0:
+                    nc.scalar.activation(
+                        out=x_norm[:, g, :], in_=xt_banks[g][:], func=ACT.Identity,
+                        scale=gain, bias=shift,
+                    )
+                else:
+                    nc.vector.tensor_scalar(
+                        out=x_norm[:, g, :], in0=xt_banks[g][:], scalar1=gain, scalar2=shift,
+                        op0=ALU.mult, op1=ALU.add,
+                    )
+
+            x_grouped = head.tile([P, PASSES, T, PACK], BF16, align_bytes=64)
+            for c in range(PASSES):
+                regroup(
+                    nc.vector.tensor_copy,
+                    x_grouped[:, c, :, :],
+                    x_norm[:, c * PACK : (c + 1) * PACK, :],
+                )
+            quantise_part(0)
+            x_codes = keep.tile([P, PASSES * T], U32, align_bytes=64)
+            x_scales = keep.tile([P, PASSES * T], U8, align_bytes=64)
+            nc.vector.quantize_mx(
+                out=x_codes[:].bitcast(FP8X4),
+                scales=x_scales[:],
+                in_=x_grouped[:].rearrange("p c n t -> p (c n t)"),
             )
-        x_codes = keep.tile([P, PASSES * T], U32, align_bytes=64)
-        x_scales = keep.tile([P, PASSES * T], U8, align_bytes=64)
-        nc.vector.quantize_mx(
-            out=x_codes[:].bitcast(FP8X4),
-            scales=x_scales[:],
-            in_=x_grouped[:].rearrange("p c n t -> p (c n t)"),
-        )
+
+        stage_pool = ctx.enter_context(tc.tile_pool(name="stage", bufs=3 * TOKEN_TILES))
 
         for part in range(PARTS + 1):
             if 1 <= part < PARTS:
-                for c in range(PASSES):
-                    regroup_unit(part, c)
+                regroup_part(part)
+                quantise_part(part)
             if part < PARTS:
-                chunk = part // PARTS_PER_CHUNK
-                if part % PARTS_PER_CHUNK == PARTS_PER_CHUNK - 1 and chunk + CHUNKS_AHEAD < CHUNKS:
-                    load_chunk(chunk + CHUNKS_AHEAD)
-                for c in range(PASSES):
-                    if (part, c) not in codes:
-                        quantise_unit(part, c)
                 multiply(part)
             if part >= 1:
                 add_bias_and_store(part - 1)
+                loads_read = PASSES * (min(part + 1, PARTS) // PARTS_PER_LOAD)
+                if part % PARTS_PER_STORE == 0 and len(raw) < min(LOADS, LOADS_AHEAD + loads_read):
+                    load_w(len(raw), 0, 1)

@@ -30,6 +30,8 @@ STORE_COLS = 1024
 STORES = N // STORE_COLS
 PARTS_PER_STORE = STORE_COLS // N_TILE
 RUN = 4
+REGROUP_AHEAD = 2
+HEAD_PAIRS = 4
 GPSIMD_EVERY = 2
 BN_FMAX = 512
 BN_STATS_DIM = 6
@@ -108,11 +110,6 @@ def tile_stulayer_pa_kernel(tc, src, ln1_w, ln1_b, w_uvqk, b_uvqk, out):
             ident = keep.tile([P, P], F32)
             make_identity(nc, ident[:])
 
-            ln_cols_ps = psum.tile([P, P], BF16, tag="bank")
-            nc.tensor.transpose(ln_cols_ps[:], ln_rows[:], ident_bf[:])
-            gain_shift = keep.tile([P, 2 * GROUPS], F32)
-            nc.vector.tensor_copy(out=gain_shift[:], in_=ln_cols_ps[:, 0 : 2 * GROUPS])
-
             bias_all = keep.tile([P, N], BF16)
 
             def spread_bias(pair):
@@ -135,7 +132,7 @@ def tile_stulayer_pa_kernel(tc, src, ln1_w, ln1_b, w_uvqk, b_uvqk, out):
             std = keep.tile([P, TOKEN_TILES], F32)
             rstd = keep.tile([P, TOKEN_TILES], F32)
             neg_mean = keep.tile([P, TOKEN_TILES], F32)
-            xhat_tiles = []
+            xt_banks = []
 
             def statistics(i):
                 for h in range(D // BN_FMAX):
@@ -150,7 +147,7 @@ def tile_stulayer_pa_kernel(tc, src, ln1_w, ln1_b, w_uvqk, b_uvqk, out):
                     bias=eps_col[:, 0:1], scale=1.0,
                 )
 
-            def normalise(i):
+            def normalise_and_transpose(i):
                 nc.vector.reciprocal(out=rstd[:, i : i + 1], in_=std[:, i : i + 1])
                 nc.vector.tensor_scalar(
                     out=neg_mean[:, i : i + 1], in0=mean_var[:, i, 0:1], scalar1=-1.0, scalar2=None,
@@ -166,28 +163,29 @@ def tile_stulayer_pa_kernel(tc, src, ln1_w, ln1_b, w_uvqk, b_uvqk, out):
                     op0=ALU.add,
                     op1=ALU.mult,
                 )
-                xhat_tiles.append(xhat_i)
+                for g in range(GROUPS):
+                    nc.tensor.transpose(
+                        xt_banks[g][:, i * P : (i + 1) * P], xhat_i[:, g * P : (g + 1) * P], ident[:]
+                    )
 
-            pairs_per_tile = PARTS // 2 // TOKEN_TILES
-            for i in range(TOKEN_TILES):
-                statistics(i)
-                for pair in range(i * pairs_per_tile, (i + 1) * pairs_per_tile):
-                    spread_bias(pair)
-                if i >= 1:
-                    normalise(i - 1)
-            normalise(TOKEN_TILES - 1)
-
-            xt_banks = []
+            ln_cols_ps = psum.tile([P, P], BF16, tag="bank")
+            nc.tensor.transpose(ln_cols_ps[:], ln_rows[:], ident_bf[:])
+            statistics(0)
+            gain_shift = keep.tile([P, 2 * GROUPS], F32)
+            nc.vector.tensor_copy(out=gain_shift[:], in_=ln_cols_ps[:, 0 : 2 * GROUPS])
+            for pair in range(HEAD_PAIRS // 2):
+                spread_bias(pair)
+            statistics(1)
+            for pair in range(HEAD_PAIRS // 2, HEAD_PAIRS):
+                spread_bias(pair)
             for g in range(GROUPS):
                 xt_g = psum.tile([P, T], F32, name="xt%d" % g, tag="bank")
                 xt_banks.append(xt_g)
-            for i in range(TOKEN_TILES):
-                for g in range(GROUPS):
-                    nc.tensor.transpose(
-                        xt_banks[g][:, i * P : (i + 1) * P],
-                        xhat_tiles[i][:, g * P : (g + 1) * P],
-                        ident[:],
-                    )
+            normalise_and_transpose(0)
+            for i in range(2, TOKEN_TILES):
+                statistics(i)
+                normalise_and_transpose(i - 1)
+            normalise_and_transpose(TOKEN_TILES - 1)
 
             grouped = {}
             codes = {}
@@ -204,7 +202,7 @@ def tile_stulayer_pa_kernel(tc, src, ln1_w, ln1_b, w_uvqk, b_uvqk, out):
                 first = (part % PARTS_PER_LOAD) * N_TILE
                 for c in range(PASSES):
                     number = (part // PARTS_PER_LOAD) * PASSES + c
-                    if c == PASSES - 1 and part % GPSIMD_EVERY == 0:
+                    if c == PASSES - 1 and part % GPSIMD_EVERY == GPSIMD_EVERY - 1:
                         copy = gpsimd_copy
                     else:
                         copy = nc.scalar.copy
@@ -222,16 +220,15 @@ def tile_stulayer_pa_kernel(tc, src, ln1_w, ln1_b, w_uvqk, b_uvqk, out):
                 codes[part] = (w_codes, w_scales)
 
             def multiply(part):
+                w_codes, w_scales = codes[part]
                 for i in range(TOKEN_TILES):
                     acc_i = psum.tile([P, N_TILE], F32, name="acc_i", tag="bank")
                     accs[(part, i)] = acc_i
-                w_codes, w_scales = codes[part]
-                for c in range(PASSES):
-                    columns = slice(c * N_TILE, (c + 1) * N_TILE)
-                    for i in range(TOKEN_TILES):
+                    for c in range(PASSES):
+                        columns = slice(c * N_TILE, (c + 1) * N_TILE)
                         tokens = slice(c * T + i * P, c * T + (i + 1) * P)
                         nc.tensor.matmul_mx(
-                            out=accs[(part, i)][:],
+                            out=acc_i[:],
                             lhsT=x_codes[:, tokens].bitcast(FP8X4),
                             lhsT_scale=x_scales[:, tokens],
                             rhs=w_codes[:, columns].bitcast(FP8X4),
@@ -268,6 +265,7 @@ def tile_stulayer_pa_kernel(tc, src, ln1_w, ln1_b, w_uvqk, b_uvqk, out):
                         )
 
             regroup_part(0)
+            quantise_part(0)
 
             x_norm = head.tile([P, GROUPS, T], BF16)
             for g in range(GROUPS):
@@ -283,6 +281,7 @@ def tile_stulayer_pa_kernel(tc, src, ln1_w, ln1_b, w_uvqk, b_uvqk, out):
                         out=x_norm[:, g, :], in0=xt_banks[g][:], scalar1=gain, scalar2=shift,
                         op0=ALU.mult, op1=ALU.add,
                     )
+            regroup_part(1)
 
             x_grouped = head.tile([P, PASSES, T, PACK], BF16, align_bytes=64)
             for c in range(PASSES):
@@ -291,7 +290,6 @@ def tile_stulayer_pa_kernel(tc, src, ln1_w, ln1_b, w_uvqk, b_uvqk, out):
                     x_grouped[:, c, :, :],
                     x_norm[:, c * PACK : (c + 1) * PACK, :],
                 )
-            quantise_part(0)
             x_codes = keep.tile([P, PASSES * T], U32, align_bytes=64)
             x_scales = keep.tile([P, PASSES * T], U8, align_bytes=64)
             nc.vector.quantize_mx(
@@ -303,13 +301,16 @@ def tile_stulayer_pa_kernel(tc, src, ln1_w, ln1_b, w_uvqk, b_uvqk, out):
         stage_pool = ctx.enter_context(tc.tile_pool(name="stage", bufs=3 * TOKEN_TILES))
 
         for part in range(PARTS + 1):
+            if part + REGROUP_AHEAD < PARTS:
+                regroup_part(part + REGROUP_AHEAD)
             if 1 <= part < PARTS:
-                regroup_part(part)
                 quantise_part(part)
             if part < PARTS:
                 multiply(part)
             if part >= 1:
                 add_bias_and_store(part - 1)
-                loads_read = PASSES * (min(part + 1, PARTS) // PARTS_PER_LOAD)
+                loads_read = PASSES * (min(part + REGROUP_AHEAD + 1, PARTS) // PARTS_PER_LOAD)
                 if part % PARTS_PER_STORE == 0 and len(raw) < min(LOADS, LOADS_AHEAD + loads_read):
                     load_w(len(raw), 0, 1)
+            if part % 2 == 1 and HEAD_PAIRS <= (part + 1) // 2 < PARTS // 2:
+                spread_bias((part + 1) // 2)

@@ -29,9 +29,11 @@ LOADS_AHEAD = 6
 STORE_COLS = 1024
 STORES = N // STORE_COLS
 PARTS_PER_STORE = STORE_COLS // N_TILE
+STORES_BY_PART = 2
 RUN = 4
 REGROUP_AHEAD = 2
-HEAD_PAIRS = 4
+SCALAR_PART = PARTS - 1
+BLOCKS = N_TILE // P
 GPSIMD_EVERY = 2
 BN_FMAX = 512
 BN_STATS_DIM = 6
@@ -98,6 +100,10 @@ def tile_stulayer_pa_kernel(tc, src, ln1_w, ln1_b, w_uvqk, b_uvqk, out):
                     nc.sync.dma_start(
                         out=ln_rows[GROUPS : 2 * GROUPS, :], in_=ln1_b.rearrange("(g p) -> g p", p=P)
                     )
+                    nc.sync.dma_start(
+                        out=ln_rows[2 * GROUPS : 2 * GROUPS + BLOCKS, :],
+                        in_=b_uvqk[SCALAR_PART * N_TILE : N].rearrange("(r p) -> r p", p=P),
+                    )
             for piece in range(2):
                 for number in range(PASSES):
                     load_w(number, piece, 2)
@@ -110,12 +116,16 @@ def tile_stulayer_pa_kernel(tc, src, ln1_w, ln1_b, w_uvqk, b_uvqk, out):
             ident = keep.tile([P, P], F32)
             make_identity(nc, ident[:])
 
+            ln_cols_ps = psum.tile([P, P], BF16, tag="bank")
+            nc.tensor.transpose(ln_cols_ps[:], ln_rows[:], ident_bf[:])
+            gain_shift = keep.tile([P, 2 * GROUPS + BLOCKS], F32)
+
             bias_all = keep.tile([P, N], BF16)
 
             def spread_bias(pair):
                 bias_ps = psum.tile([P, 2 * N_TILE], BF16, tag="bank")
-                for half in range(2):
-                    r = 2 * pair + half
+                rows = [r for r in (2 * pair, 2 * pair + 1) if r != SCALAR_PART]
+                for half, r in enumerate(rows):
                     nc.tensor.matmul(
                         out=bias_ps[:, half * N_TILE : (half + 1) * N_TILE],
                         lhsT=ident_bf[:, r : r + 1].to_broadcast([P, P]),
@@ -123,16 +133,16 @@ def tile_stulayer_pa_kernel(tc, src, ln1_w, ln1_b, w_uvqk, b_uvqk, out):
                         start=True,
                         stop=True,
                     )
-                nc.scalar.copy(
-                    out=bias_all[:, pair * 2 * N_TILE : (pair + 1) * 2 * N_TILE], in_=bias_ps[:]
-                )
+                width = len(rows) * N_TILE
+                first = pair * 2 * N_TILE
+                nc.scalar.copy(out=bias_all[:, first : first + width], in_=bias_ps[:, 0:width])
 
             stats = keep.tile([P, TOKEN_TILES, D // BN_FMAX, BN_STATS_DIM], F32)
             mean_var = keep.tile([P, TOKEN_TILES, BN_AGGR_DIM], F32)
             std = keep.tile([P, TOKEN_TILES], F32)
             rstd = keep.tile([P, TOKEN_TILES], F32)
             neg_mean = keep.tile([P, TOKEN_TILES], F32)
-            xt_banks = []
+            xhat_tiles = []
 
             def statistics(i):
                 for h in range(D // BN_FMAX):
@@ -147,7 +157,7 @@ def tile_stulayer_pa_kernel(tc, src, ln1_w, ln1_b, w_uvqk, b_uvqk, out):
                     bias=eps_col[:, 0:1], scale=1.0,
                 )
 
-            def normalise_and_transpose(i):
+            def normalise(i):
                 nc.vector.reciprocal(out=rstd[:, i : i + 1], in_=std[:, i : i + 1])
                 nc.vector.tensor_scalar(
                     out=neg_mean[:, i : i + 1], in0=mean_var[:, i, 0:1], scalar1=-1.0, scalar2=None,
@@ -163,29 +173,32 @@ def tile_stulayer_pa_kernel(tc, src, ln1_w, ln1_b, w_uvqk, b_uvqk, out):
                     op0=ALU.add,
                     op1=ALU.mult,
                 )
-                for g in range(GROUPS):
-                    nc.tensor.transpose(
-                        xt_banks[g][:, i * P : (i + 1) * P], xhat_i[:, g * P : (g + 1) * P], ident[:]
-                    )
+                xhat_tiles.append(xhat_i)
 
-            ln_cols_ps = psum.tile([P, P], BF16, tag="bank")
-            nc.tensor.transpose(ln_cols_ps[:], ln_rows[:], ident_bf[:])
-            statistics(0)
-            gain_shift = keep.tile([P, 2 * GROUPS], F32)
-            nc.vector.tensor_copy(out=gain_shift[:], in_=ln_cols_ps[:, 0 : 2 * GROUPS])
-            for pair in range(HEAD_PAIRS // 2):
-                spread_bias(pair)
-            statistics(1)
-            for pair in range(HEAD_PAIRS // 2, HEAD_PAIRS):
-                spread_bias(pair)
+            pairs_per_tile = PARTS // 2 // TOKEN_TILES
+            for i in range(TOKEN_TILES):
+                statistics(i)
+                if i == 0:
+                    nc.vector.tensor_copy(
+                        out=gain_shift[:], in_=ln_cols_ps[:, 0 : 2 * GROUPS + BLOCKS]
+                    )
+                for pair in range(i * pairs_per_tile, (i + 1) * pairs_per_tile):
+                    spread_bias(pair)
+                if i >= 1:
+                    normalise(i - 1)
+            normalise(TOKEN_TILES - 1)
+
+            xt_banks = []
             for g in range(GROUPS):
                 xt_g = psum.tile([P, T], F32, name="xt%d" % g, tag="bank")
                 xt_banks.append(xt_g)
-            normalise_and_transpose(0)
-            for i in range(2, TOKEN_TILES):
-                statistics(i)
-                normalise_and_transpose(i - 1)
-            normalise_and_transpose(TOKEN_TILES - 1)
+            for i in range(TOKEN_TILES):
+                for g in range(GROUPS):
+                    nc.tensor.transpose(
+                        xt_banks[g][:, i * P : (i + 1) * P],
+                        xhat_tiles[i][:, g * P : (g + 1) * P],
+                        ident[:],
+                    )
 
             grouped = {}
             codes = {}
@@ -202,7 +215,7 @@ def tile_stulayer_pa_kernel(tc, src, ln1_w, ln1_b, w_uvqk, b_uvqk, out):
                 first = (part % PARTS_PER_LOAD) * N_TILE
                 for c in range(PASSES):
                     number = (part // PARTS_PER_LOAD) * PASSES + c
-                    if c == PASSES - 1 and part % GPSIMD_EVERY == GPSIMD_EVERY - 1:
+                    if c == PASSES - 1 and part % GPSIMD_EVERY == 0:
                         copy = gpsimd_copy
                     else:
                         copy = nc.scalar.copy
@@ -237,6 +250,45 @@ def tile_stulayer_pa_kernel(tc, src, ln1_w, ln1_b, w_uvqk, b_uvqk, out):
                             stop=(c == PASSES - 1),
                         )
 
+            def multiply_transposed(part):
+                w_codes, w_scales = codes[part]
+                for b in range(BLOCKS):
+                    acc_b = psum.tile([P, T], F32, name="acc_b", tag="bank")
+                    accs[(part, b)] = acc_b
+                    for c in range(PASSES):
+                        columns = slice(c * N_TILE + b * P, c * N_TILE + (b + 1) * P)
+                        tokens = slice(c * T, (c + 1) * T)
+                        nc.tensor.matmul_mx(
+                            out=acc_b[:],
+                            lhsT=w_codes[:, columns].bitcast(FP8X4),
+                            lhsT_scale=w_scales[:, columns],
+                            rhs=x_codes[:, tokens].bitcast(FP8X4),
+                            rhs_scale=x_scales[:, tokens],
+                            start=(c == 0),
+                            stop=(c == PASSES - 1),
+                        )
+
+            def scalar_add_bias_and_store(part):
+                sums = []
+                for b in range(BLOCKS):
+                    sums_b = turn_pool.tile([P, T], F32, name="sums_b", tag="sums")
+                    nc.scalar.activation(
+                        out=sums_b[:], in_=accs[(part, b)][:], func=ACT.Identity,
+                        bias=gain_shift[:, 2 * GROUPS + b : 2 * GROUPS + b + 1], scale=1.0,
+                    )
+                    sums.append(sums_b)
+                turned = turned_pool.tile([P, TOKEN_TILES, N_TILE], F32)
+                for b in range(BLOCKS):
+                    back = psum.tile([P, TOKEN_TILES, P], F32, tag="bank")
+                    for i in range(TOKEN_TILES):
+                        nc.tensor.transpose(back[:, i, :], sums[b][:, i * P : (i + 1) * P], ident[:])
+                    nc.scalar.copy(out=turned[:, :, b * P : (b + 1) * P], in_=back[:])
+                for i in range(TOKEN_TILES):
+                    nc.sync.dma_start(
+                        out=out_rows[i * P : (i + 1) * P, part * N_TILE : (part + 1) * N_TILE],
+                        in_=turned[:, i, :],
+                    )
+
             def add_bias_and_store(part):
                 store = part // PARTS_PER_STORE
                 local = (part % PARTS_PER_STORE) * N_TILE
@@ -253,7 +305,7 @@ def tile_stulayer_pa_kernel(tc, src, ln1_w, ln1_b, w_uvqk, b_uvqk, out):
                         in1=bias_all[:, first : first + N_TILE],
                         op=ALU.add,
                     )
-                    if store == STORES - 1:
+                    if store >= STORES - STORES_BY_PART:
                         nc.sync.dma_start(
                             out=out_rows[token_rows, first : first + N_TILE],
                             in_=stage[:, local : local + N_TILE],
@@ -265,7 +317,6 @@ def tile_stulayer_pa_kernel(tc, src, ln1_w, ln1_b, w_uvqk, b_uvqk, out):
                         )
 
             regroup_part(0)
-            quantise_part(0)
 
             x_norm = head.tile([P, GROUPS, T], BF16)
             for g in range(GROUPS):
@@ -281,7 +332,6 @@ def tile_stulayer_pa_kernel(tc, src, ln1_w, ln1_b, w_uvqk, b_uvqk, out):
                         out=x_norm[:, g, :], in0=xt_banks[g][:], scalar1=gain, scalar2=shift,
                         op0=ALU.mult, op1=ALU.add,
                     )
-            regroup_part(1)
 
             x_grouped = head.tile([P, PASSES, T, PACK], BF16, align_bytes=64)
             for c in range(PASSES):
@@ -290,6 +340,7 @@ def tile_stulayer_pa_kernel(tc, src, ln1_w, ln1_b, w_uvqk, b_uvqk, out):
                     x_grouped[:, c, :, :],
                     x_norm[:, c * PACK : (c + 1) * PACK, :],
                 )
+            quantise_part(0)
             x_codes = keep.tile([P, PASSES * T], U32, align_bytes=64)
             x_scales = keep.tile([P, PASSES * T], U8, align_bytes=64)
             nc.vector.quantize_mx(
@@ -299,18 +350,27 @@ def tile_stulayer_pa_kernel(tc, src, ln1_w, ln1_b, w_uvqk, b_uvqk, out):
             )
 
         stage_pool = ctx.enter_context(tc.tile_pool(name="stage", bufs=3 * TOKEN_TILES))
+        turn_pool = ctx.enter_context(tc.tile_pool(name="turn", bufs=BLOCKS))
+        turned_pool = ctx.enter_context(tc.tile_pool(name="turned", bufs=1))
 
-        for part in range(PARTS + 1):
-            if part + REGROUP_AHEAD < PARTS:
-                regroup_part(part + REGROUP_AHEAD)
-            if 1 <= part < PARTS:
-                quantise_part(part)
-            if part < PARTS:
-                multiply(part)
-            if part >= 1:
-                add_bias_and_store(part - 1)
-                loads_read = PASSES * (min(part + REGROUP_AHEAD + 1, PARTS) // PARTS_PER_LOAD)
-                if part % PARTS_PER_STORE == 0 and len(raw) < min(LOADS, LOADS_AHEAD + loads_read):
+        order = list(range(PARTS - 3)) + [SCALAR_PART, PARTS - 3, PARTS - 2]
+        for step in range(1, REGROUP_AHEAD):
+            regroup_part(order[step])
+        for step in range(PARTS + 1):
+            if step + REGROUP_AHEAD < PARTS:
+                regroup_part(order[step + REGROUP_AHEAD])
+            if 1 <= step < PARTS:
+                quantise_part(order[step])
+            if step >= 1:
+                if order[step - 1] == SCALAR_PART:
+                    scalar_add_bias_and_store(order[step - 1])
+                else:
+                    add_bias_and_store(order[step - 1])
+                loads_read = PASSES * (min(step + 1, PARTS) // PARTS_PER_LOAD)
+                if step % PARTS_PER_STORE == 0 and len(raw) < min(LOADS, LOADS_AHEAD + loads_read):
                     load_w(len(raw), 0, 1)
-            if part % 2 == 1 and HEAD_PAIRS <= (part + 1) // 2 < PARTS // 2:
-                spread_bias((part + 1) // 2)
+            if step < PARTS:
+                if order[step] == SCALAR_PART:
+                    multiply_transposed(order[step])
+                else:
+                    multiply(order[step])

from contextlib import ExitStack

import concourse.mybir as mybir
from concourse.masks import make_identity

F32 = mybir.dt.float32
BF16 = mybir.dt.bfloat16
U32 = mybir.dt.uint32
U8 = mybir.dt.uint8
FP8X4 = mybir.dt.float8_e4m3fn_x4
ALU = mybir.AluOpType
ACT = mybir.ActivationFunctionType

P = 128
PACK = 4
T = 512
D = 1024
N = 8192
EPS = 1e-5
PASSES = D // (P * PACK)
GROUPS = PASSES * PACK
TOKEN_TILES = T // P
N_TILE = 512
PARTS = N // N_TILE
LOAD_COLS = 2048
PARTS_PER_LOAD = LOAD_COLS // N_TILE
LOADS = (N // LOAD_COLS) * PASSES
LOADS_AHEAD = 6
STORE_COLS = 1024
STORES = N // STORE_COLS
PARTS_PER_STORE = STORE_COLS // N_TILE
STORES_BY_PART = 2
RUN = 4
REGROUP_AHEAD = 2
SCALAR_PART = PARTS - 1
BLOCKS = N_TILE // P
GPSIMD_EVERY = 2
BN_FMAX = 512
BN_STATS_DIM = 6
BN_AGGR_DIM = 2

FLOPS = 2 * T * D * N


def regroup(engine_copy, grouped, rows):
    engine_copy(
        out=grouped.rearrange("p (q i) t -> p q t i", i=RUN),
        in_=rows.rearrange("p t (q i) -> p q t i", i=RUN),
    )


def tile_stulayer_pa_kernel(tc, src, ln1_w, ln1_b, w_uvqk, b_uvqk, out):
    nc = tc.nc
    src_rows = src.rearrange("t b d -> (t b) d")
    out_rows = out.rearrange("t b n -> (t b) n")
    w_view = w_uvqk.rearrange("(c t p) n -> p c t n", c=PASSES, t=PACK, p=P)

    with ExitStack() as ctx:
        keep = ctx.enter_context(tc.tile_pool(name="keep", bufs=1))
        raw_pool = ctx.enter_context(tc.tile_pool(name="raw", bufs=LOADS_AHEAD))
        grouped_pool = ctx.enter_context(tc.tile_pool(name="grouped", bufs=3))
        code_pool = ctx.enter_context(tc.tile_pool(name="codes", bufs=4))
        psum = ctx.enter_context(tc.psum_pool(name="psum", bufs=8))
        ctx.enter_context(tc.manual_schedule())

        raw = []

        def load_w(number, piece, pieces):
            if piece == 0:
                raw_tile = raw_pool.tile([P, PACK, LOAD_COLS], BF16, name="raw_tile", tag="raw")
                raw.append(raw_tile)
            width = LOAD_COLS // pieces
            local = piece * width
            first = (number // PASSES) * LOAD_COLS + local
            nc.sync.dma_start(
                out=raw[number][:, :, local : local + width],
                in_=w_view[:, number % PASSES, :, first : first + width],
            )

        with tc.tile_pool(name="head", bufs=1) as head:

            ln_rows = keep.tile([P, P], BF16)
            nc.vector.memset(ln_rows[:], 0.0)
            bias_rows = keep.tile([P, N_TILE], BF16)
            nc.vector.memset(bias_rows[:], 0.0)
            eps_col = keep.tile([P, 1], F32)
            nc.vector.memset(eps_col[:], EPS)
            x_tiles = []
            for i in range(TOKEN_TILES):
                x_i = head.tile([P, D], BF16, name="x%d" % i)
                nc.sync.dma_start(out=x_i[:], in_=src_rows[i * P : (i + 1) * P, :])
                x_tiles.append(x_i)
                if i == 0:
                    nc.sync.dma_start(
                        out=bias_rows[0:PARTS, :], in_=b_uvqk.rearrange("(r n) -> r n", n=N_TILE)
                    )
                    nc.sync.dma_start(
                        out=ln_rows[0:GROUPS, :], in_=ln1_w.rearrange("(g p) -> g p", p=P)
                    )
                    nc.sync.dma_start(
                        out=ln_rows[GROUPS : 2 * GROUPS, :], in_=ln1_b.rearrange("(g p) -> g p", p=P)
                    )
                    nc.sync.dma_start(
                        out=ln_rows[2 * GROUPS : 2 * GROUPS + BLOCKS, :],
                        in_=b_uvqk[SCALAR_PART * N_TILE : N].rearrange("(r p) -> r p", p=P),
                    )
            for piece in range(2):
                for number in range(PASSES):
                    load_w(number, piece, 2)
            for number in range(PASSES, LOADS_AHEAD):
                load_w(number, 0, 1)


            ident_bf = keep.tile([P, P], BF16)
            make_identity(nc, ident_bf[:])
            ident = keep.tile([P, P], F32)
            make_identity(nc, ident[:])

            ln_cols_ps = psum.tile([P, P], BF16, tag="bank")
            nc.tensor.transpose(ln_cols_ps[:], ln_rows[:], ident_bf[:])
            gain_shift = keep.tile([P, 2 * GROUPS + BLOCKS], F32)

            bias_all = keep.tile([P, N], BF16)

            def spread_bias(pair):
                bias_ps = psum.tile([P, 2 * N_TILE], BF16, tag="bank")
                rows = [r for r in (2 * pair, 2 * pair + 1) if r != SCALAR_PART]
                for half, r in enumerate(rows):
                    nc.tensor.matmul(
                        out=bias_ps[:, half * N_TILE : (half + 1) * N_TILE],
                        lhsT=ident_bf[:, r : r + 1].to_broadcast([P, P]),
                        rhs=bias_rows[:],
                        start=True,
                        stop=True,
                    )
                width = len(rows) * N_TILE
                first = pair * 2 * N_TILE
                nc.scalar.copy(out=bias_all[:, first : first + width], in_=bias_ps[:, 0:width])

            stats = keep.tile([P, TOKEN_TILES, D // BN_FMAX, BN_STATS_DIM], F32)
            mean_var = keep.tile([P, TOKEN_TILES, BN_AGGR_DIM], F32)
            std = keep.tile([P, TOKEN_TILES], F32)
            rstd = keep.tile([P, TOKEN_TILES], F32)
            neg_mean = keep.tile([P, TOKEN_TILES], F32)
            xhat_tiles = []

            def statistics(i):
                for h in range(D // BN_FMAX):
                    nc.vector.bn_stats(
                        out=stats[:, i, h, :], in_=x_tiles[i][:, h * BN_FMAX : (h + 1) * BN_FMAX]
                    )
                nc.vector.bn_aggr(
                    out=mean_var[:, i, :], in_=stats[:, i, :, :].rearrange("p h s -> p (h s)")
                )
                nc.scalar.activation(
                    out=std[:, i : i + 1], in_=mean_var[:, i, 1:2], func=ACT.Sqrt,
                    bias=eps_col[:, 0:1], scale=1.0,
                )

            def normalise(i):
                nc.vector.reciprocal(out=rstd[:, i : i + 1], in_=std[:, i : i + 1])
                nc.vector.tensor_scalar(
                    out=neg_mean[:, i : i + 1], in0=mean_var[:, i, 0:1], scalar1=-1.0, scalar2=None,
                    op0=ALU.mult,
                )
                xhat_i = head.tile([P, D], F32, name="xhat%d" % i)
                engine = nc.vector if i == TOKEN_TILES - 1 else nc.gpsimd
                engine.tensor_scalar(
                    out=xhat_i[:],
                    in0=x_tiles[i][:],
                    scalar1=neg_mean[:, i : i + 1],
                    scalar2=rstd[:, i : i + 1],
                    op0=ALU.add,
                    op1=ALU.mult,
                )
                xhat_tiles.append(xhat_i)

            pairs_per_tile = PARTS // 2 // TOKEN_TILES
            for i in range(TOKEN_TILES):
                statistics(i)
                if i == 0:
                    nc.vector.tensor_copy(
                        out=gain_shift[:], in_=ln_cols_ps[:, 0 : 2 * GROUPS + BLOCKS]
                    )
                for pair in range(i * pairs_per_tile, (i + 1) * pairs_per_tile):
                    spread_bias(pair)
                if i >= 1:
                    normalise(i - 1)
            normalise(TOKEN_TILES - 1)

            xt_banks = []
            for g in range(GROUPS):
                xt_g = psum.tile([P, T], F32, name="xt%d" % g, tag="bank")
                xt_banks.append(xt_g)
            for i in range(TOKEN_TILES):
                for g in range(GROUPS):
                    nc.tensor.transpose(
                        xt_banks[g][:, i * P : (i + 1) * P],
                        xhat_tiles[i][:, g * P : (g + 1) * P],
                        ident[:],
                    )

            grouped = {}
            codes = {}
            accs = {}
            stages = {}

            def gpsimd_copy(out, in_):
                nc.gpsimd.tensor_scalar(
                    out=out, in0=in_, scalar1=1.0, scalar2=0.0, op0=ALU.mult, op1=ALU.add
                )

            def regroup_part(part):
                w_grouped = grouped_pool.tile([P, PASSES, N_TILE, PACK], BF16, align_bytes=64)
                first = (part % PARTS_PER_LOAD) * N_TILE
                for c in range(PASSES):
                    number = (part // PARTS_PER_LOAD) * PASSES + c
                    if c == PASSES - 1 and part % GPSIMD_EVERY == 0:
                        copy = gpsimd_copy
                    else:
                        copy = nc.scalar.copy
                    regroup(copy, w_grouped[:, c, :, :], raw[number][:, :, first : first + N_TILE])
                grouped[part] = w_grouped

            def quantise_part(part):
                w_codes = code_pool.tile([P, PASSES * N_TILE], U32, align_bytes=64)
                w_scales = code_pool.tile([P, PASSES * N_TILE], U8, align_bytes=64)
                nc.vector.quantize_mx(
                    out=w_codes[:].bitcast(FP8X4),
                    scales=w_scales[:],
                    in_=grouped[part][:].rearrange("p c n t -> p (c n t)"),
                )
                codes[part] = (w_codes, w_scales)

            def multiply(part):
                w_codes, w_scales = codes[part]
                for i in range(TOKEN_TILES):
                    acc_i = psum.tile([P, N_TILE], F32, name="acc_i", tag="bank")
                    accs[(part, i)] = acc_i
                    for c in range(PASSES):
                        columns = slice(c * N_TILE, (c + 1) * N_TILE)
                        tokens = slice(c * T + i * P, c * T + (i + 1) * P)
                        nc.tensor.matmul_mx(
                            out=acc_i[:],
                            lhsT=x_codes[:, tokens].bitcast(FP8X4),
                            lhsT_scale=x_scales[:, tokens],
                            rhs=w_codes[:, columns].bitcast(FP8X4),
                            rhs_scale=w_scales[:, columns],
                            start=(c == 0),
                            stop=(c == PASSES - 1),
                        )

            def multiply_transposed(part):
                w_codes, w_scales = codes[part]
                for b in range(BLOCKS):
                    acc_b = psum.tile([P, T], F32, name="acc_b", tag="bank")
                    accs[(part, b)] = acc_b
                    for c in range(PASSES):
                        columns = slice(c * N_TILE + b * P, c * N_TILE + (b + 1) * P)
                        tokens = slice(c * T, (c + 1) * T)
                        nc.tensor.matmul_mx(
                            out=acc_b[:],
                            lhsT=w_codes[:, columns].bitcast(FP8X4),
                            lhsT_scale=w_scales[:, columns],
                            rhs=x_codes[:, tokens].bitcast(FP8X4),
                            rhs_scale=x_scales[:, tokens],
                            start=(c == 0),
                            stop=(c == PASSES - 1),
                        )

            def scalar_add_bias_and_store(part):
                sums = []
                for b in range(BLOCKS):
                    sums_b = turn_pool.tile([P, T], F32, name="sums_b", tag="sums")
                    nc.scalar.activation(
                        out=sums_b[:], in_=accs[(part, b)][:], func=ACT.Identity,
                        bias=gain_shift[:, 2 * GROUPS + b : 2 * GROUPS + b + 1], scale=1.0,
                    )
                    sums.append(sums_b)
                turned = turned_pool.tile([P, TOKEN_TILES, N_TILE], F32)
                for b in range(BLOCKS):
                    back = psum.tile([P, TOKEN_TILES, P], F32, tag="bank")
                    for i in range(TOKEN_TILES):
                        nc.tensor.transpose(back[:, i, :], sums[b][:, i * P : (i + 1) * P], ident[:])
                    nc.scalar.copy(out=turned[:, :, b * P : (b + 1) * P], in_=back[:])
                for i in range(TOKEN_TILES):
                    nc.sync.dma_start(
                        out=out_rows[i * P : (i + 1) * P, part * N_TILE : (part + 1) * N_TILE],
                        in_=turned[:, i, :],
                    )

            def add_bias_and_store(part):
                store = part // PARTS_PER_STORE
                local = (part % PARTS_PER_STORE) * N_TILE
                first = part * N_TILE
                for i in range(TOKEN_TILES):
                    if local == 0:
                        stage_i = stage_pool.tile([P, STORE_COLS], F32, name="stage_i", tag="stage")
                        stages[(store, i)] = stage_i
                    stage = stages[(store, i)]
                    token_rows = slice(i * P, (i + 1) * P)
                    nc.vector.tensor_tensor(
                        out=stage[:, local : local + N_TILE],
                        in0=accs[(part, i)][:],
                        in1=bias_all[:, first : first + N_TILE],
                        op=ALU.add,
                    )
                    if store >= STORES - STORES_BY_PART:
                        nc.sync.dma_start(
                            out=out_rows[token_rows, first : first + N_TILE],
                            in_=stage[:, local : local + N_TILE],
                        )
                    elif local + N_TILE == STORE_COLS:
                        nc.sync.dma_start(
                            out=out_rows[token_rows, store * STORE_COLS : (store + 1) * STORE_COLS],
                            in_=stage[:],
                        )

            regroup_part(0)

            x_norm = head.tile([P, GROUPS, T], BF16)
            for g in range(GROUPS):
                gain = gain_shift[:, g : g + 1]
                shift = gain_shift[:, GROUPS + g : GROUPS + g + 1]
                if g % 2 == 0:
                    nc.scalar.activation(
                        out=x_norm[:, g, :], in_=xt_banks[g][:], func=ACT.Identity,
                        scale=gain, bias=shift,
                    )
                else:
                    nc.vector.tensor_scalar(
                        out=x_norm[:, g, :], in0=xt_banks[g][:], scalar1=gain, scalar2=shift,
                        op0=ALU.mult, op1=ALU.add,
                    )

            x_grouped = head.tile([P, PASSES, T, PACK], BF16, align_bytes=64)
            for c in range(PASSES):
                regroup(
                    nc.vector.tensor_copy,
                    x_grouped[:, c, :, :],
                    x_norm[:, c * PACK : (c + 1) * PACK, :],
                )
            quantise_part(0)
            x_codes = keep.tile([P, PASSES * T], U32, align_bytes=64)
            x_scales = keep.tile([P, PASSES * T], U8, align_bytes=64)
            nc.vector.quantize_mx(
                out=x_codes[:].bitcast(FP8X4),
                scales=x_scales[:],
                in_=x_grouped[:].rearrange("p c n t -> p (c n t)"),
            )

        stage_pool = ctx.enter_context(tc.tile_pool(name="stage", bufs=3 * TOKEN_TILES))
        turn_pool = ctx.enter_context(tc.tile_pool(name="turn", bufs=BLOCKS))
        turned_pool = ctx.enter_context(tc.tile_pool(name="turned", bufs=1))

        order = list(range(PARTS - 3)) + [SCALAR_PART, PARTS - 3, PARTS - 2]
        for step in range(1, REGROUP_AHEAD):
            regroup_part(order[step])
        for step in range(PARTS + 1):
            if step + REGROUP_AHEAD < PARTS:
                regroup_part(order[step + REGROUP_AHEAD])
            if 1 <= step < PARTS:
                quantise_part(order[step])
            if step >= 1:
                if order[step - 1] == SCALAR_PART:
                    scalar_add_bias_and_store(order[step - 1])
                else:
                    add_bias_and_store(order[step - 1])
                loads_read = PASSES * (min(step + 1, PARTS) // PARTS_PER_LOAD)
                if step % PARTS_PER_STORE == 0 and len(raw) < min(LOADS, LOADS_AHEAD + loads_read):
                    load_w(len(raw), 0, 1)
            if step < PARTS:
                if order[step] == SCALAR_PART:
                    multiply_transposed(order[step])
                else:
                    multiply(order[step])
